import numpy as np
import ml_dtypes

BF16 = ml_dtypes.bfloat16


def bf(x):
    return np.asarray(x, np.float32).astype(BF16)


def f32(x):
    return np.asarray(x, np.float32)


def f64(x):
    return np.asarray(x).astype(np.float64)


def striped(idx):
    return np.tile(idx.reshape(-1, 16).T, (8, 1))


V, E, NI, P, M, T, L, N = 256, 128, 128, 4, 512, 64, 8, 512
LOGIT_SCALE = np.log(1.0 / 0.07)


def setup_inputs():
    return {"table": bf(0.125 * np.random.standard_normal((V, E))), "img": bf(np.random.standard_normal((E, M)) / np.sqrt(E)), "text_len": f32(1 + np.random.permutation(T) % L).reshape(1, T), "offs": striped(np.random.permutation(np.tile(np.arange(V), 2))[:N])}


def reference(table, img, text_len, offs):
    idx = offs[:16].T.reshape(-1)
    sims = f64(img).T @ f64(table)[idx].T
    best = sims.reshape(P, NI, N).max(axis=0)
    total = best.reshape(NI, T, L).sum(axis=2)
    return total / f64(text_len) * np.exp(LOGIT_SCALE)

@@ -1,0 +1,86 @@
+import math
+
+import concourse.mybir as mybir
+from concourse.masks import make_identity
+
+BF16, F32, U16 = mybir.dt.bfloat16, mybir.dt.float32, mybir.dt.uint16
+
+WORDS = 256
+FEATURES = 128
+IMAGES = 128
+PATCHES = 4
+TEXTS = 64
+TEXT_WORDS = 8
+LISTED = TEXTS * TEXT_WORDS
+LOGIT_SCALE = math.exp(math.log(1.0 / 0.07))
+
+PIECE = WORDS
+PIECES = LISTED // PIECE
+PIECE_TEXTS = PIECE // TEXT_WORDS
+PIECE_OFFSET_COLUMNS = PIECE // 16
+
+FLOPS = 2 * FEATURES * PATCHES * IMAGES * LISTED
+
+
+def tile_multimodalmodel_kernel(tc, table, img, text_len, offs, out):
+    nc = tc.nc
+    with (
+        tc.tile_pool(name="held", bufs=1) as held,
+        tc.tile_pool(name="work", bufs=2) as work,
+        tc.psum_pool(name="flip", bufs=1) as flip,
+        tc.psum_pool(name="sims", bufs=2) as sims,
+    ):
+        word_rows = held.tile([128, WORDS // 128, FEATURES], BF16, name="word_rows")
+        nc.sync.dma_start(word_rows[:], table.rearrange("(b w) e -> w b e", w=128))
+        offsets = held.tile([128, LISTED // 16], U16, name="offsets")
+        nc.sync.dma_start(offsets[:], offs)
+        patches = held.tile([FEATURES, PATCHES * IMAGES], BF16, name="patches")
+        nc.scalar.dma_start(patches[:], img)
+        lengths = held.tile([IMAGES, TEXTS], F32, name="lengths")
+        nc.scalar.dma_start(lengths[:], text_len.broadcast_to([IMAGES, TEXTS]))
+
+        identity = held.tile([128, 128], BF16, name="identity")
+        make_identity(nc, identity[:])
+        flipped = flip.tile([FEATURES, WORDS], BF16, name="flipped")
+        for b in range(WORDS // 128):
+            nc.tensor.transpose(flipped[:, b * 128 : (b + 1) * 128], word_rows[:, b, :], identity[:])
+        words = held.tile([FEATURES, WORDS], BF16, name="words")
+        nc.scalar.copy(words[:], flipped[:])
+
+        weight = held.tile([IMAGES, TEXTS], F32, name="weight")
+        nc.vector.reciprocal(weight[:], lengths[:])
+        nc.vector.tensor_scalar_mul(weight[:], weight[:], LOGIT_SCALE)
+
+        totals = held.tile([IMAGES, TEXTS], F32, name="totals")
+        scores = held.tile([IMAGES, TEXTS], F32, name="scores")
+        for h in range(PIECES):
+            texts = slice(h * PIECE_TEXTS, (h + 1) * PIECE_TEXTS)
+            piece = offsets[:, h * PIECE_OFFSET_COLUMNS : (h + 1) * PIECE_OFFSET_COLUMNS]
+
+            sim_01 = sims.tile([IMAGES, 2, PIECE], F32, name="sim_01")
+            sim_23 = sims.tile([IMAGES, 2, PIECE], F32, name="sim_23")
+            for p in range(PATCHES):
+                bank = sim_01 if p < 2 else sim_23
+                nc.tensor.matmul(
+                    bank[:, p % 2, :],
+                    patches[:, p * IMAGES : (p + 1) * IMAGES],
+                    words[:].indirect(piece),
+                    start=True,
+                    stop=True,
+                )
+
+            copy_01 = work.tile([IMAGES, 2, PIECE], F32, name="copy_01")
+            nc.scalar.copy(copy_01[:], sim_01[:])
+            best_of_two = work.tile([IMAGES, 2, PIECE], F32, name="best_of_two")
+            nc.vector.tensor_max(best_of_two[:], copy_01[:], sim_23[:])
+            best = work.tile([IMAGES, PIECE], F32, name="best")
+            nc.vector.tensor_max(best[:], best_of_two[:, 0, :], best_of_two[:, 1, :])
+
+            nc.vector.reduce_sum(
+                totals[:, texts],
+                best[:].rearrange("i (t l) -> i t l", l=TEXT_WORDS),
+                axis=mybir.AxisListType.X,
+            )
+
+            nc.vector.tensor_mul(scores[:, texts], totals[:, texts], weight[:, texts])
+            nc.sync.dma_start(out[:, texts], scores[:, texts])

@@ -27,6 +27,7 @@ def tile_multimodalmodel_kernel(tc, table, img, text_len, offs, out):
     with (
         tc.tile_pool(name="held", bufs=1) as held,
         tc.tile_pool(name="work", bufs=2) as work,
+        tc.tile_pool(name="turn", bufs=1) as turn,
         tc.psum_pool(name="flip", bufs=1) as flip,
         tc.psum_pool(name="sims", bufs=2) as sims,
     ):
@@ -46,10 +47,6 @@ def tile_multimodalmodel_kernel(tc, table, img, text_len, offs, out):
             nc.tensor.transpose(flipped[:, b * 128 : (b + 1) * 128], word_rows[:, b, :], identity[:])
         words = held.tile([FEATURES, WORDS], BF16, name="words")
         nc.scalar.copy(words[:], flipped[:])
-
-        weight = held.tile([IMAGES, TEXTS], F32, name="weight")
-        nc.vector.reciprocal(weight[:], lengths[:])
-        nc.vector.tensor_scalar_mul(weight[:], weight[:], LOGIT_SCALE)
 
         totals = held.tile([IMAGES, TEXTS], F32, name="totals")
         scores = held.tile([IMAGES, TEXTS], F32, name="scores")
@@ -71,10 +68,15 @@ def tile_multimodalmodel_kernel(tc, table, img, text_len, offs, out):
 
             copy_01 = work.tile([IMAGES, 2, PIECE], F32, name="copy_01")
             nc.scalar.copy(copy_01[:], sim_01[:])
-            best_of_two = work.tile([IMAGES, 2, PIECE], F32, name="best_of_two")
+            pool, tag = (turn, "turn") if h == 0 else (work, "best_of_two")
+            best_of_two = pool.tile([IMAGES, 2, PIECE], F32, name="best_of_two", tag=tag)
             nc.vector.tensor_max(best_of_two[:], copy_01[:], sim_23[:])
             best = work.tile([IMAGES, PIECE], F32, name="best")
             nc.vector.tensor_max(best[:], best_of_two[:, 0, :], best_of_two[:, 1, :])
+
+            if h == 0:
+                inverse = turn.tile([IMAGES, TEXTS], F32, name="inverse", tag="turn")
+                nc.vector.reciprocal(inverse[:], lengths[:])
 
             nc.vector.reduce_sum(
                 totals[:, texts],
@@ -82,5 +84,12 @@ def tile_multimodalmodel_kernel(tc, table, img, text_len, offs, out):
                 axis=mybir.AxisListType.X,
             )
 
-            nc.vector.tensor_mul(scores[:, texts], totals[:, texts], weight[:, texts])
+            nc.vector.scalar_tensor_tensor(
+                scores[:, texts],
+                totals[:, texts],
+                LOGIT_SCALE,
+                inverse[:, texts],
+                op0=mybir.AluOpType.mult,
+                op1=mybir.AluOpType.mult,
+            )
             nc.sync.dma_start(out[:, texts], scores[:, texts])

@@ -26,10 +26,9 @@ def tile_multimodalmodel_kernel(tc, table, img, text_len, offs, out):
     nc = tc.nc
     with (
         tc.tile_pool(name="held", bufs=1) as held,
-        tc.tile_pool(name="work", bufs=2) as work,
-        tc.tile_pool(name="turn", bufs=1) as turn,
+        tc.tile_pool(name="work", bufs=1) as work,
         tc.psum_pool(name="flip", bufs=1) as flip,
-        tc.psum_pool(name="sims", bufs=2) as sims,
+        tc.psum_pool(name="sims", bufs=1) as sims,
     ):
         word_rows = held.tile([128, WORDS // 128, FEATURES], BF16, name="word_rows")
         nc.sync.dma_start(word_rows[:], table.rearrange("(b w) e -> w b e", w=128))
@@ -50,40 +49,38 @@ def tile_multimodalmodel_kernel(tc, table, img, text_len, offs, out):
 
         totals = held.tile([IMAGES, TEXTS], F32, name="totals")
         scores = held.tile([IMAGES, TEXTS], F32, name="scores")
-        for h in range(PIECES):
-            texts = slice(h * PIECE_TEXTS, (h + 1) * PIECE_TEXTS)
-            piece = offsets[:, h * PIECE_OFFSET_COLUMNS : (h + 1) * PIECE_OFFSET_COLUMNS]
-
-            sim_01 = sims.tile([IMAGES, 2, PIECE], F32, name="sim_01")
-            sim_23 = sims.tile([IMAGES, 2, PIECE], F32, name="sim_23")
-            for p in range(PATCHES):
-                bank = sim_01 if p < 2 else sim_23
+        running = [None] * PIECES
+        for p in range(PATCHES):
+            for h in range(PIECES):
+                piece = offsets[:, h * PIECE_OFFSET_COLUMNS : (h + 1) * PIECE_OFFSET_COLUMNS]
+                slot = (p * PIECES + h) % 7
+                sim = sims.tile([IMAGES, 2, PIECE], F32, name=f"sim_{p}_{h}", tag=f"bank_{slot}")
                 nc.tensor.matmul(
-                    bank[:, p % 2, :],
+                    sim[:, 0, :],
                     patches[:, p * IMAGES : (p + 1) * IMAGES],
                     words[:].indirect(piece),
                     start=True,
                     stop=True,
                 )
+                best = work.tile([IMAGES, PIECE], F32, name=f"best_{p}_{h}")
+                if p == 0:
+                    nc.scalar.copy(best[:], sim[:, 0, :])
+                else:
+                    nc.vector.tensor_max(best[:], running[h][:], sim[:, 0, :])
+                running[h] = best
 
-            copy_01 = work.tile([IMAGES, 2, PIECE], F32, name="copy_01")
-            nc.scalar.copy(copy_01[:], sim_01[:])
-            pool, tag = (turn, "turn") if h == 0 else (work, "best_of_two")
-            best_of_two = pool.tile([IMAGES, 2, PIECE], F32, name="best_of_two", tag=tag)
-            nc.vector.tensor_max(best_of_two[:], copy_01[:], sim_23[:])
-            best = work.tile([IMAGES, PIECE], F32, name="best")
-            nc.vector.tensor_max(best[:], best_of_two[:, 0, :], best_of_two[:, 1, :])
+        inverse = work.tile([IMAGES, TEXTS], F32, name="inverse", tag=f"best_{PATCHES - 2}_0")
+        nc.vector.reciprocal(inverse[:], lengths[:])
 
-            if h == 0:
-                inverse = turn.tile([IMAGES, TEXTS], F32, name="inverse", tag="turn")
-                nc.vector.reciprocal(inverse[:], lengths[:])
-
+        totals = held.tile([IMAGES, TEXTS], F32, name="totals")
+        scores = held.tile([IMAGES, TEXTS], F32, name="scores")
+        for h in range(PIECES):
+            texts = slice(h * PIECE_TEXTS, (h + 1) * PIECE_TEXTS)
             nc.vector.reduce_sum(
                 totals[:, texts],
-                best[:].rearrange("i (t l) -> i t l", l=TEXT_WORDS),
+                running[h][:].rearrange("i (t l) -> i t l", l=TEXT_WORDS),
                 axis=mybir.AxisListType.X,
             )
-
             nc.vector.scalar_tensor_tensor(
                 scores[:, texts],
                 totals[:, texts],

import math

import concourse.mybir as mybir
from concourse.masks import make_identity

BF16, F32, U16 = mybir.dt.bfloat16, mybir.dt.float32, mybir.dt.uint16

WORDS = 256
FEATURES = 128
IMAGES = 128
PATCHES = 4
TEXTS = 64
TEXT_WORDS = 8
LISTED = TEXTS * TEXT_WORDS
LOGIT_SCALE = math.exp(math.log(1.0 / 0.07))

PIECE = WORDS
PIECES = LISTED // PIECE
PIECE_TEXTS = PIECE // TEXT_WORDS
PIECE_OFFSET_COLUMNS = PIECE // 16

FLOPS = 2 * FEATURES * PATCHES * IMAGES * LISTED


def tile_multimodalmodel_kernel(tc, table, img, text_len, offs, out):
    nc = tc.nc
    with (
        tc.tile_pool(name="held", bufs=1) as held,
        tc.tile_pool(name="work", bufs=1) as work,
        tc.psum_pool(name="flip", bufs=1) as flip,
        tc.psum_pool(name="sims", bufs=1) as sims,
    ):
        word_rows = held.tile([128, WORDS // 128, FEATURES], BF16, name="word_rows")
        nc.sync.dma_start(word_rows[:], table.rearrange("(b w) e -> w b e", w=128))
        offsets = held.tile([128, LISTED // 16], U16, name="offsets")
        nc.sync.dma_start(offsets[:], offs)
        patches = held.tile([FEATURES, PATCHES * IMAGES], BF16, name="patches")
        nc.scalar.dma_start(patches[:], img)
        lengths = held.tile([IMAGES, TEXTS], F32, name="lengths")
        nc.scalar.dma_start(lengths[:], text_len.broadcast_to([IMAGES, TEXTS]))

        identity = held.tile([128, 128], BF16, name="identity")
        make_identity(nc, identity[:])
        flipped = flip.tile([FEATURES, WORDS], BF16, name="flipped")
        for b in range(WORDS // 128):
            nc.tensor.transpose(flipped[:, b * 128 : (b + 1) * 128], word_rows[:, b, :], identity[:])
        words = held.tile([FEATURES, WORDS], BF16, name="words")
        nc.scalar.copy(words[:], flipped[:])

        totals = held.tile([IMAGES, TEXTS], F32, name="totals")
        scores = held.tile([IMAGES, TEXTS], F32, name="scores")
        running = [None] * PIECES
        for p in range(PATCHES):
            for h in range(PIECES):
                piece = offsets[:, h * PIECE_OFFSET_COLUMNS : (h + 1) * PIECE_OFFSET_COLUMNS]
                slot = (p * PIECES + h) % 7
                sim = sims.tile([IMAGES, 2, PIECE], F32, name=f"sim_{p}_{h}", tag=f"bank_{slot}")
                nc.tensor.matmul(
                    sim[:, 0, :],
                    patches[:, p * IMAGES : (p + 1) * IMAGES],
                    words[:].indirect(piece),
                    start=True,
                    stop=True,
                )
                best = work.tile([IMAGES, PIECE], F32, name=f"best_{p}_{h}")
                if p == 0:
                    nc.scalar.copy(best[:], sim[:, 0, :])
                else:
                    nc.vector.tensor_max(best[:], running[h][:], sim[:, 0, :])
                running[h] = best

        inverse = work.tile([IMAGES, TEXTS], F32, name="inverse", tag=f"best_{PATCHES - 2}_0")
        nc.vector.reciprocal(inverse[:], lengths[:])

        totals = held.tile([IMAGES, TEXTS], F32, name="totals")
        scores = held.tile([IMAGES, TEXTS], F32, name="scores")
        for h in range(PIECES):
            texts = slice(h * PIECE_TEXTS, (h + 1) * PIECE_TEXTS)
            nc.vector.reduce_sum(
                totals[:, texts],
                running[h][:].rearrange("i (t l) -> i t l", l=TEXT_WORDS),
                axis=mybir.AxisListType.X,
            )
            nc.vector.scalar_tensor_tensor(
                scores[:, texts],
                totals[:, texts],
                LOGIT_SCALE,
                inverse[:, texts],
                op0=mybir.AluOpType.mult,
                op1=mybir.AluOpType.mult,
            )
            nc.sync.dma_start(out[:, texts], scores[:, texts])
